import numpy as np
import ml_dtypes


def mxq(x, axis, fmt="e4m3"):
    dtype, down = {"e4m3": (ml_dtypes.float8_e4m3fn, 7), "e5m2": (ml_dtypes.float8_e5m2, 14)}[fmt]
    v = np.moveaxis(np.asarray(x, np.float32).astype(ml_dtypes.bfloat16).astype(np.float64), axis, -1)
    blocks = v.reshape(v.shape[:-1] + (-1, 32))
    amax = np.abs(blocks).max(-1, keepdims=True)
    byte = np.maximum(np.where(amax > 0, np.frexp(amax)[1] - 1 + 127, 0) - down, 1)
    scale = np.exp2(byte - 127.0)
    codes = (blocks / scale).astype(np.float32).astype(dtype).astype(np.float64)
    return np.moveaxis((codes * scale).reshape(v.shape), -1, axis)


WIDE = False


def mx_kscale(k):
    if not WIDE:
        return np.ones(k)
    levels = np.array([20, -20, 10, -10, 0])
    a = np.random.permutation(np.resize(levels, k // 512 * 4)).reshape(k // 512, 4)
    idx = np.arange(k)
    return np.exp2(a[idx // 512, idx % 128 // 32])


BF16 = ml_dtypes.bfloat16


def bf(x):
    return np.asarray(x, np.float32).astype(BF16)


def f64(x):
    return np.asarray(x).astype(np.float64)


IN_F, OUT_F = 512, 512
GRID_SIZE, SPLINE_ORDER = 5, 3
NUM_BASIS = 10
GRID_LO, GRID_HI = -1.0, 1.0
SCALE_LOGISTIC = 1.0
B = 1024
G_SCALE = 4.0


def sigmoid(v):
    return 1.0 / (1.0 + np.exp(-v))


def knots():
    h = (GRID_HI - GRID_LO) / GRID_SIZE
    return np.arange(-SPLINE_ORDER, GRID_SIZE + SPLINE_ORDER + 1, dtype=np.float64) * h + GRID_LO


def b_splines(x, t, order):
    xe = x[:, :, None]
    bases = ((xe >= t[:-1]) & (xe < t[1:])).astype(np.float64)
    for k in range(1, order + 1):
        bases = ((xe - t[:-(k + 1)]) / (t[k:-1] - t[:-(k + 1)]) * bases[:, :, :-1]
                 + (t[k + 1:] - xe) / (t[k + 1:] - t[1:-k]) * bases[:, :, 1:])
    return bases


def setup_inputs():
    u = mx_kscale(OUT_F)
    x = np.random.standard_normal((B, IN_F))
    base_weight = np.random.standard_normal((OUT_F, IN_F)) * 0.06 / u[:, None]
    spline_weight = np.random.standard_normal((OUT_F, IN_F, GRID_SIZE + SPLINE_ORDER)) * 0.2
    spline_scaler = np.random.standard_normal((OUT_F, IN_F)) * 0.3 / u[:, None]
    a = np.random.standard_normal((IN_F, NUM_BASIS))
    b = np.random.standard_normal((IN_F, NUM_BASIS))
    logistic_weight = np.random.standard_normal((OUT_F, IN_F * NUM_BASIS)) * 0.01
    logistic_scaler = (1.0 + 0.1 * np.random.standard_normal(OUT_F)) / u
    g = np.random.standard_normal((B, OUT_F)) * np.exp2(np.random.randint(-12, 1, (B, 1))) * G_SCALE * u[None, :]
    return {
        "x": bf(x),
        "base_weight": bf(base_weight),
        "spline_weight": bf(spline_weight),
        "spline_scaler": bf(spline_scaler),
        "a": bf(a),
        "b": bf(b),
        "logistic_weight": bf(logistic_weight),
        "logistic_scaler": bf(logistic_scaler),
        "grad_out": bf(g),
    }


def reference(x, base_weight, spline_weight, spline_scaler, a, b, logistic_weight, logistic_scaler, grad_out):
    x = f64(x)
    a = f64(a)
    b = f64(b)
    rows = x.shape[0]
    nb = GRID_SIZE + SPLINE_ORDER

    gq = mxq(f64(grad_out), 1, "e5m2")
    sw = (f64(spline_weight) * f64(spline_scaler)[:, :, None]).reshape(OUT_F, IN_F * nb)
    lw = f64(logistic_weight) * SCALE_LOGISTIC * f64(logistic_scaler)[:, None]
    p_base = gq @ mxq(f64(base_weight), 0, "e4m3")
    p_spline = (gq @ mxq(sw, 0, "e4m3")).reshape(rows, IN_F, nb)
    p_logistic = (gq @ mxq(lw, 0, "e4m3")).reshape(rows, IN_F, NUM_BASIS)

    s = sigmoid(x)
    d_silu = s * (1.0 + x * (1.0 - s))
    t = knots()
    n2 = b_splines(x, t, SPLINE_ORDER - 1)
    d_bases = (SPLINE_ORDER / (t[SPLINE_ORDER:-1] - t[:-(SPLINE_ORDER + 1)]) * n2[:, :, :-1]
               - SPLINE_ORDER / (t[SPLINE_ORDER + 1:] - t[1:-SPLINE_ORDER]) * n2[:, :, 1:])
    sg = sigmoid(a * (x[:, :, None] - b))
    d_phi = 2.0 * a * sg * (1.0 - sg)

    return d_silu * p_base + (d_bases * p_spline).sum(axis=2) + (d_phi * p_logistic).sum(axis=2)

@@ -1,0 +1,319 @@
+from contextlib import ExitStack
+
+import concourse.mybir as mybir
+from concourse.masks import make_identity
+
+F32 = mybir.dt.float32
+BF16 = mybir.dt.bfloat16
+U32 = mybir.dt.uint32
+U8 = mybir.dt.uint8
+E4X4 = mybir.dt.float8_e4m3fn_x4
+E5X4 = mybir.dt.float8_e5m2_x4
+ALU = mybir.AluOpType
+ACT = mybir.ActivationFunctionType
+
+P = 128
+ROWS = 1024
+FEAT = 512
+NG = 8
+NL = 10
+NCH = 1 + NG + NL
+HALF = 512
+BUNCH = 3
+FLOPS = 2 * ROWS * 512 * (FEAT * NCH)
+
+
+def tile_kanlinear_kernel(
+    tc, x, base_weight, spline_weight, spline_scaler, a, b, logistic_weight, logistic_scaler, grad_out, out
+):
+    nc = tc.nc
+    with ExitStack() as ctx:
+        const = ctx.enter_context(tc.tile_pool(name="const", bufs=1))
+        wts = ctx.enter_context(tc.tile_pool(name="wts", bufs=2))
+        psum = ctx.enter_context(tc.psum_pool(name="psum", bufs=6))
+        psacc = ctx.enter_context(tc.psum_pool(name="psacc", bufs=2))
+
+        ident_b = const.tile([P, P], BF16, name="ident_b")
+        make_identity(nc, ident_b[:])
+        ident_f = const.tile([P, P], F32, name="ident_f")
+        make_identity(nc, ident_f[:])
+
+        x_t = const.tile([P, 4, ROWS], F32, name="x_t")
+        g_codes = const.tile([P, ROWS], U32, name="g_codes", align_bytes=64)
+        g_scales = const.tile([P, ROWS], U8, name="g_scales", align_bytes=64)
+        a_sb = const.tile([P, 4, NL], BF16, name="a_sb")
+        b_sb = const.tile([P, 4, NL], BF16, name="b_sb")
+        a_half = const.tile([P, 4 * NL], F32, name="a_half")
+        a_nhalf = const.tile([P, 4 * NL], F32, name="a_nhalf")
+        t_bias = const.tile([P, 4 * NL], F32, name="t_bias")
+        l_scal = const.tile([P, 4], BF16, name="l_scal")
+
+        raw = {}
+        quant = {}
+
+        def load_weights(ic):
+            rb = wts.tile([P, 4, P], BF16, tag="rb", name="rb")
+            nc.sync.dma_start(
+                out=rb[:], in_=base_weight.rearrange("(t p) i -> p t i", p=P)[:, :, ic * P : (ic + 1) * P]
+            )
+            ss = wts.tile([P, 4, P], BF16, tag="ss", name="ss")
+            nc.sync.dma_start(
+                out=ss[:], in_=spline_scaler.rearrange("(t p) i -> p t i", p=P)[:, :, ic * P : (ic + 1) * P]
+            )
+            rs = wts.tile([P, 4, P * NG], BF16, tag="rs", name="rs")
+            nc.sync.dma_start(
+                out=rs[:],
+                in_=spline_weight.rearrange("(t p) i g -> p t (i g)", p=P)[:, :, ic * P * NG : (ic + 1) * P * NG],
+            )
+            rl = wts.tile([P, 4, P * NL], BF16, tag="rl", name="rl")
+            nc.sync.dma_start(
+                out=rl[:],
+                in_=logistic_weight.rearrange("(t p) c -> p t c", p=P)[:, :, ic * P * NL : (ic + 1) * P * NL],
+            )
+            raw[ic] = (rb, ss, rs, rl)
+
+        def prep_weights(ic):
+            rb, ss, rs, rl = raw[ic]
+            grp = wts.tile([P, NCH * P * 4], BF16, tag="grp", name="grp", bufs=1, align_bytes=64)
+            wc = wts.tile([P, NCH * P], U32, tag="wc", name="wc", align_bytes=64)
+            ws = wts.tile([P, NCH * P], U8, tag="ws", name="ws", align_bytes=64)
+            e0 = P * 4
+            e1 = e0 + NG * P * 4
+            e2 = e1 + NL * P * 4
+            nc.vector.tensor_copy(
+                out=grp[:, 0:e0].rearrange("p (i t) -> p i t", t=4), in_=rb[:].rearrange("p t i -> p i t")
+            )
+            nc.vector.tensor_tensor(
+                out=grp[:, e0:e1].rearrange("p (g i t) -> p g i t", g=NG, t=4),
+                in0=rs[:].rearrange("p t (i g) -> p g i t", g=NG),
+                in1=ss[:].rearrange("p t i -> p i t").unsqueeze(1).to_broadcast([P, NG, P, 4]),
+                op=ALU.mult,
+            )
+            nc.vector.tensor_tensor(
+                out=grp[:, e1:e2].rearrange("p (n i t) -> p n i t", n=NL, t=4),
+                in0=rl[:].rearrange("p t (i n) -> p n i t", n=NL),
+                in1=l_scal[:].unsqueeze(1).unsqueeze(1).to_broadcast([P, NL, P, 4]),
+                op=ALU.mult,
+            )
+            for lo, hi in ((0, e0), (e0, e1), (e1, e1 + 4096), (e1 + 4096, e2)):
+                nc.vector.quantize_mx(
+                    out=wc[:, lo // 4 : hi // 4].bitcast(E4X4), scales=ws[:, lo // 4 : hi // 4], in_=grp[:, lo:hi]
+                )
+            quant[ic] = (wc, ws)
+
+        with tc.tile_pool(name="prep", bufs=1) as prep:
+            g_sb = prep.tile([P, 8, 512], BF16, name="g_sb")
+            nc.sync.dma_start(out=g_sb[:], in_=grad_out.rearrange("(t p) o -> p t o", p=P))
+            x_sb = prep.tile([P, 8, FEAT], BF16, name="x_sb")
+            nc.sync.dma_start(out=x_sb[:], in_=x.rearrange("(t p) i -> p t i", p=P))
+            ls_rows = prep.tile([P, P], BF16, name="ls_rows")
+            nc.vector.memset(ls_rows[:], 0.0)
+            nc.sync.dma_start(out=ls_rows[0:4, :], in_=logistic_scaler.rearrange("(t p) -> t p", p=P))
+            nc.sync.dma_start(out=a_sb[:], in_=a.rearrange("(c p) n -> p c n", p=P))
+            nc.sync.dma_start(out=b_sb[:], in_=b.rearrange("(c p) n -> p c n", p=P))
+            load_weights(0)
+            load_weights(1)
+
+            ls_ps = psum.tile([P, P], BF16, tag="mx", name="ls_ps")
+            nc.tensor.transpose(ls_ps[:], ls_rows[:], ident_b[:])
+            nc.vector.tensor_copy(out=l_scal[:], in_=ls_ps[:, 0:4])
+
+            gg = prep.tile([P, ROWS, 4], BF16, name="gg", align_bytes=64)
+            for rt in range(8):
+                pt = psum.tile([P, 4, P], BF16, tag="mx", name="pt")
+                for t in range(4):
+                    nc.tensor.transpose(pt[:, t, :], g_sb[:, rt, t * P : (t + 1) * P], ident_b[:])
+                if rt % 2 == 0:
+                    nc.vector.tensor_copy(out=gg[:, rt * P : (rt + 1) * P, :], in_=pt[:].rearrange("p t r -> p r t"))
+                else:
+                    nc.scalar.copy(out=gg[:, rt * P : (rt + 1) * P, :], in_=pt[:].rearrange("p t r -> p r t"))
+            for rh in range(2):
+                nc.vector.quantize_mx(
+                    out=g_codes[:, rh * HALF : (rh + 1) * HALF].bitcast(E5X4),
+                    scales=g_scales[:, rh * HALF : (rh + 1) * HALF],
+                    in_=gg[:, rh * HALF : (rh + 1) * HALF, :].rearrange("p r t -> p (r t)"),
+                )
+
+            for ic in range(4):
+                px = psum.tile([P, 8, P], BF16, tag="mx", name="px")
+                for rt in range(8):
+                    nc.tensor.transpose(px[:, rt, :], x_sb[:, rt, ic * P : (ic + 1) * P], ident_b[:])
+                nc.scalar.copy(out=x_t[:, ic, :], in_=px[:].rearrange("p t r -> p (t r)"))
+
+            nc.vector.tensor_scalar(
+                out=a_half[:], in0=a_sb[:].rearrange("p c n -> p (c n)"), scalar1=0.5, scalar2=None, op0=ALU.mult
+            )
+            nc.vector.tensor_scalar(
+                out=a_nhalf[:], in0=a_sb[:].rearrange("p c n -> p (c n)"), scalar1=-0.5, scalar2=None, op0=ALU.mult
+            )
+            nc.vector.tensor_tensor(
+                out=t_bias[:], in0=a_nhalf[:], in1=b_sb[:].rearrange("p c n -> p (c n)"), op=ALU.mult
+            )
+            prep_weights(0)
+
+        work = ctx.enter_context(tc.tile_pool(name="work", bufs=2))
+        planes = {}
+
+        def merge(dst, src):
+            nc.vector.scalar_tensor_tensor(
+                out=dst[:], in0=src[:], scalar=-2.0, in1=dst[:], op0=ALU.mult, op1=ALU.add
+            )
+
+        def gen_spline(ic, m):
+            xi = x_t[:, ic, :]
+            c = work.tile([P, ROWS], F32, tag="sp", name="c", bufs=11)
+            nc.gpsimd.tensor_scalar(out=c[:], in0=xi, scalar1=2.5, scalar2=4.5 - m, op0=ALU.mult, op1=ALU.add)
+            nc.gpsimd.tensor_scalar(out=c[:], in0=c[:], scalar1=1.0, scalar2=-1.0, op0=ALU.min, op1=ALU.max)
+            ab = work.tile([P, ROWS], F32, tag="ab", name="ab", bufs=2)
+            nc.scalar.activation(out=ab[:], in_=c[:], func=ACT.Abs)
+            nc.vector.scalar_tensor_tensor(
+                out=c[:], in0=ab[:], scalar=2.0, in1=c[:], op0=ALU.subtract, op1=ALU.mult
+            )
+            sp = planes[ic]["sp"]
+            sp[m] = c
+            if m == 1:
+                merge(sp[0], sp[1])
+            if m == 2:
+                merge(sp[1], sp[2])
+            if m == 9:
+                merge(sp[9], sp[8])
+                merge(sp[8], sp[7])
+
+        def gen_logistic(ic, n):
+            k = ic * NL + n
+            t = work.tile([P, ROWS], F32, tag="lg", name="t", bufs=11)
+            nc.scalar.activation(
+                out=t[:], in_=x_t[:, ic, :], func=ACT.Tanh, bias=t_bias[:, k : k + 1], scale=a_half[:, k : k + 1]
+            )
+            nc.scalar.activation(out=t[:], in_=t[:], func=ACT.Square)
+            nc.gpsimd.tensor_scalar(
+                out=t[:], in0=t[:], scalar1=a_nhalf[:, k : k + 1], scalar2=a_half[:, k : k + 1],
+                op0=ALU.mult, op1=ALU.add,
+            )
+            planes[ic]["lg"][n] = t
+
+        def gen_base(ic):
+            xi = x_t[:, ic, :]
+            th = work.tile([P, ROWS], F32, tag="th", name="th", bufs=1)
+            nc.scalar.activation(out=th[:], in_=xi, func=ACT.Tanh, scale=0.5)
+            ds = work.tile([P, ROWS], F32, tag="ds", name="ds", bufs=2)
+            nc.scalar.activation(out=ds[:], in_=th[:], func=ACT.Square)
+            nc.vector.tensor_scalar(out=ds[:], in0=ds[:], scalar1=-0.25, scalar2=0.25, op0=ALU.mult, op1=ALU.add)
+            nc.vector.tensor_tensor(out=ds[:], in0=ds[:], in1=xi, op=ALU.mult)
+            nc.vector.scalar_tensor_tensor(
+                out=ds[:], in0=th[:], scalar=0.5, in1=ds[:], op0=ALU.mult, op1=ALU.add
+            )
+            planes[ic]["ds"] = ds
+
+        def new_planes(ic):
+            planes[ic] = {"sp": [None] * 10, "lg": [None] * NL, "ds": None}
+
+        units = [((1, ), "sp", 0, -1.25, 0), ((2, ), "sp", 1, -1.25, 1), ((3, 1), "sp", 2, -1.25, 2)]
+        for m in range(3, 7):
+            units.append(((1 + m, m - 1), "sp", m, -1.25, None))
+            units.append(((m, ), "sp", m, 2.5, m))
+        units.append(((8, 6), "sp", 7, -1.25, 7))
+        units.append(((7, ), "sp", 8, -1.25, 8))
+        units.append(((8, ), "sp", 9, -1.25, 9))
+        for n in range(NL):
+            units.append(((1 + NG + n, ), "lg", n, None, n))
+        units.append(((0, ), "ds", 0, 0.5, 0))
+        n_units = len(units)
+
+        todo = [(ic, rh, u) for ic in range(4) for rh in range(2) for u in range(n_units)]
+        bunches = [todo[k : k + BUNCH] for k in range(0, len(todo), BUNCH)]
+        banks = {}
+        prods = {}
+        accs = {}
+
+        def emit_mx(job):
+            ic, rh, u = job
+            wc, ws = quant[ic]
+            chs = units[u][0]
+            bank = psum.tile([P, HALF], F32, tag="mx", name="bank")
+            for j, ch in enumerate(chs):
+                nc.tensor.matmul_mx(
+                    out=bank[:],
+                    lhsT=wc[:, ch * P : (ch + 1) * P].bitcast(E4X4),
+                    lhsT_scale=ws[:, ch * P : (ch + 1) * P],
+                    rhs=g_codes[:, rh * HALF : (rh + 1) * HALF].bitcast(E5X4),
+                    rhs_scale=g_scales[:, rh * HALF : (rh + 1) * HALF],
+                    start=(j == 0),
+                    stop=(j == len(chs) - 1),
+                )
+            banks[job] = bank
+
+        def emit_prod(job):
+            ic, rh, u = job
+            if rh == 0 and u == 0 and ic + 1 < 4:
+                prep_weights(ic + 1)
+                if ic + 2 < 4:
+                    load_weights(ic + 2)
+                new_planes(ic + 1)
+            fam = units[u][1]
+            idx = units[u][2]
+            scal = units[u][3]
+            bank = banks[job]
+            y = work.tile([P, HALF], F32, tag="y", name="y", bufs=6)
+            cols = slice(rh * HALF, (rh + 1) * HALF)
+            if fam == "sp":
+                nc.vector.scalar_tensor_tensor(
+                    out=y[:], in0=planes[ic]["sp"][idx][:, cols], scalar=scal, in1=bank[:], op0=ALU.mult, op1=ALU.mult
+                )
+            elif fam == "lg":
+                nc.vector.tensor_tensor(out=y[:], in0=bank[:], in1=planes[ic]["lg"][idx][:, cols], op=ALU.mult)
+            else:
+                nc.vector.scalar_tensor_tensor(
+                    out=y[:], in0=planes[ic]["ds"][:, cols], scalar=scal, in1=bank[:], op0=ALU.add, op1=ALU.mult
+                )
+            prods[job] = y
+            freed = units[u][4]
+            if rh == 1 and ic + 1 < 4 and freed is not None:
+                if fam == "sp":
+                    gen_spline(ic + 1, freed)
+                elif fam == "lg":
+                    gen_logistic(ic + 1, freed)
+                else:
+                    gen_base(ic + 1)
+
+        def emit_acc(job):
+            ic, rh, u = job
+            y = prods[job]
+            if u == 0:
+                acc_new = psacc.tile([P, HALF], F32, tag="acc", name="acc_new")
+                accs[(ic, rh)] = acc_new
+            acc = accs[(ic, rh)]
+            for rt in range(4):
+                nc.tensor.matmul(
+                    out=acc[:, rt * P : (rt + 1) * P],
+                    lhsT=y[:, rt * P : (rt + 1) * P],
+                    rhs=ident_f[:],
+                    is_transpose=True,
+                    start=(u == 0 and rt == 0),
+                    stop=(u == n_units - 1 and rt == 3),
+                )
+            if u == n_units - 1:
+                ob = work.tile([P, 4, P], F32, tag="ob", name="ob", bufs=2)
+                nc.scalar.copy(out=ob[:].rearrange("p t i -> p (t i)"), in_=acc[:])
+                nc.sync.dma_start(
+                    out=out.rearrange("(t p) i -> p t i", p=P)[:, rh * 4 : (rh + 1) * 4, ic * P : (ic + 1) * P],
+                    in_=ob[:],
+                )
+
+        new_planes(0)
+        for m in range(10):
+            gen_spline(0, m)
+        for n in range(NL):
+            gen_logistic(0, n)
+        gen_base(0)
+
+        for job in bunches[0]:
+            emit_mx(job)
+        for k in range(len(bunches)):
+            if k + 1 < len(bunches):
+                for job in bunches[k + 1]:
+                    emit_mx(job)
+            for job in bunches[k]:
+                emit_prod(job)
+            for job in bunches[k]:
+                emit_acc(job)

@@ -19,7 +19,9 @@ NG = 8
 NL = 10
 NCH = 1 + NG + NL
 HALF = 512
-BUNCH = 3
+BUNCH = 2
+LOOK = 2
+N_AFFINE_ON_SCALAR = 8
 FLOPS = 2 * ROWS * 512 * (FEAT * NCH)
 
 
@@ -31,7 +33,7 @@ def tile_kanlinear_kernel(
         const = ctx.enter_context(tc.tile_pool(name="const", bufs=1))
         wts = ctx.enter_context(tc.tile_pool(name="wts", bufs=2))
         psum = ctx.enter_context(tc.psum_pool(name="psum", bufs=6))
-        psacc = ctx.enter_context(tc.psum_pool(name="psacc", bufs=2))
+        psacc = ctx.enter_context(tc.psum_pool(name="psacc", bufs=1))
 
         ident_b = const.tile([P, P], BF16, name="ident_b")
         make_identity(nc, ident_b[:])
@@ -161,13 +163,14 @@ def tile_kanlinear_kernel(
 
         def gen_spline(ic, m):
             xi = x_t[:, ic, :]
+            mid = 0.4 * m - 1.8
             c = work.tile([P, ROWS], F32, tag="sp", name="c", bufs=11)
-            nc.gpsimd.tensor_scalar(out=c[:], in0=xi, scalar1=2.5, scalar2=4.5 - m, op0=ALU.mult, op1=ALU.add)
-            nc.gpsimd.tensor_scalar(out=c[:], in0=c[:], scalar1=1.0, scalar2=-1.0, op0=ALU.min, op1=ALU.max)
-            ab = work.tile([P, ROWS], F32, tag="ab", name="ab", bufs=2)
-            nc.scalar.activation(out=ab[:], in_=c[:], func=ACT.Abs)
+            nc.vector.tensor_scalar(out=c[:], in0=xi, scalar1=mid - 0.4, scalar2=mid + 0.4, op0=ALU.max, op1=ALU.min)
+            ab = work.tile([P, ROWS], F32, tag="ab", name="ab", bufs=3)
+            nc.scalar.activation(out=ab[:], in_=c[:], func=ACT.Abs, bias=4.5 - m, scale=2.5)
+            nc.scalar.activation(out=ab[:], in_=ab[:], func=ACT.Identity, bias=-5.0, scale=2.5)
             nc.vector.scalar_tensor_tensor(
-                out=c[:], in0=ab[:], scalar=2.0, in1=c[:], op0=ALU.subtract, op1=ALU.mult
+                out=c[:], in0=c[:], scalar=mid, in1=ab[:], op0=ALU.subtract, op1=ALU.mult
             )
             sp = planes[ic]["sp"]
             sp[m] = c
@@ -186,10 +189,15 @@ def tile_kanlinear_kernel(
                 out=t[:], in_=x_t[:, ic, :], func=ACT.Tanh, bias=t_bias[:, k : k + 1], scale=a_half[:, k : k + 1]
             )
             nc.scalar.activation(out=t[:], in_=t[:], func=ACT.Square)
-            nc.gpsimd.tensor_scalar(
-                out=t[:], in0=t[:], scalar1=a_nhalf[:, k : k + 1], scalar2=a_half[:, k : k + 1],
-                op0=ALU.mult, op1=ALU.add,
-            )
+            if n < N_AFFINE_ON_SCALAR:
+                nc.scalar.activation(
+                    out=t[:], in_=t[:], func=ACT.Identity, bias=a_half[:, k : k + 1], scale=a_nhalf[:, k : k + 1]
+                )
+            else:
+                nc.vector.tensor_scalar(
+                    out=t[:], in0=t[:], scalar1=a_nhalf[:, k : k + 1], scalar2=a_half[:, k : k + 1],
+                    op0=ALU.mult, op1=ALU.add,
+                )
             planes[ic]["lg"][n] = t
 
         def gen_base(ic):
@@ -220,7 +228,7 @@ def tile_kanlinear_kernel(
         units.append(((0, ), "ds", 0, 0.5, 0))
         n_units = len(units)
 
-        todo = [(ic, rh, u) for ic in range(4) for rh in range(2) for u in range(n_units)]
+        todo = [(ic, rh, u) for ic in range(4) for u in range(n_units) for rh in range(2)]
         bunches = [todo[k : k + BUNCH] for k in range(0, len(todo), BUNCH)]
         banks = {}
         prods = {}
@@ -280,7 +288,7 @@ def tile_kanlinear_kernel(
             ic, rh, u = job
             y = prods[job]
             if u == 0:
-                acc_new = psacc.tile([P, HALF], F32, tag="acc", name="acc_new")
+                acc_new = psacc.tile([P, HALF], F32, tag="acc%d" % rh, name="acc_new")
                 accs[(ic, rh)] = acc_new
             acc = accs[(ic, rh)]
             for rt in range(4):
@@ -307,11 +315,12 @@ def tile_kanlinear_kernel(
             gen_logistic(0, n)
         gen_base(0)
 
-        for job in bunches[0]:
-            emit_mx(job)
+        for k in range(LOOK):
+            for job in bunches[k]:
+                emit_mx(job)
         for k in range(len(bunches)):
-            if k + 1 < len(bunches):
-                for job in bunches[k + 1]:
+            if k + LOOK < len(bunches):
+                for job in bunches[k + LOOK]:
                     emit_mx(job)
             for job in bunches[k]:
                 emit_prod(job)

@@ -22,6 +22,8 @@ HALF = 512
 BUNCH = 2
 LOOK = 2
 N_AFFINE_ON_SCALAR = 8
+PIECES = ((0, 1), (1, 5), (5, 9), (9, 13), (13, 17), (17, 19))
+N_STEPS = len(PIECES) + 1
 FLOPS = 2 * ROWS * 512 * (FEAT * NCH)
 
 
@@ -74,34 +76,42 @@ def tile_kanlinear_kernel(
             )
             raw[ic] = (rb, ss, rs, rl)
 
-        def prep_weights(ic):
+        def prep_weights(ic, step):
             rb, ss, rs, rl = raw[ic]
-            grp = wts.tile([P, NCH * P * 4], BF16, tag="grp", name="grp", bufs=1, align_bytes=64)
-            wc = wts.tile([P, NCH * P], U32, tag="wc", name="wc", align_bytes=64)
-            ws = wts.tile([P, NCH * P], U8, tag="ws", name="ws", align_bytes=64)
-            e0 = P * 4
-            e1 = e0 + NG * P * 4
-            e2 = e1 + NL * P * 4
-            nc.vector.tensor_copy(
-                out=grp[:, 0:e0].rearrange("p (i t) -> p i t", t=4), in_=rb[:].rearrange("p t i -> p i t")
-            )
-            nc.vector.tensor_tensor(
-                out=grp[:, e0:e1].rearrange("p (g i t) -> p g i t", g=NG, t=4),
-                in0=rs[:].rearrange("p t (i g) -> p g i t", g=NG),
-                in1=ss[:].rearrange("p t i -> p i t").unsqueeze(1).to_broadcast([P, NG, P, 4]),
-                op=ALU.mult,
-            )
-            nc.vector.tensor_tensor(
-                out=grp[:, e1:e2].rearrange("p (n i t) -> p n i t", n=NL, t=4),
-                in0=rl[:].rearrange("p t (i n) -> p n i t", n=NL),
-                in1=l_scal[:].unsqueeze(1).unsqueeze(1).to_broadcast([P, NL, P, 4]),
-                op=ALU.mult,
-            )
-            for lo, hi in ((0, e0), (e0, e1), (e1, e1 + 4096), (e1 + 4096, e2)):
+            if step == 0:
+                grp_new = wts.tile([P, NCH * P * 4], BF16, tag="grp", name="grp_new", bufs=1, align_bytes=64)
+                wc_new = wts.tile([P, NCH * P], U32, tag="wc", name="wc_new", align_bytes=64)
+                ws_new = wts.tile([P, NCH * P], U8, tag="ws", name="ws_new", align_bytes=64)
+                quant[ic] = (wc_new, ws_new, grp_new)
+            wc, ws, grp = quant[ic]
+            if step < len(PIECES):
+                c0, c1 = PIECES[step]
+                dst = grp[:, c0 * P * 4 : c1 * P * 4]
+                if c0 == 0:
+                    nc.vector.tensor_copy(
+                        out=dst.rearrange("p (i t) -> p i t", t=4), in_=rb[:].rearrange("p t i -> p i t")
+                    )
+                elif c0 < 1 + NG:
+                    nc.vector.tensor_tensor(
+                        out=dst.rearrange("p (g i t) -> p g i t", g=c1 - c0, t=4),
+                        in0=rs[:].rearrange("p t (i g) -> p g i t", g=NG)[:, c0 - 1 : c1 - 1],
+                        in1=ss[:].rearrange("p t i -> p i t").unsqueeze(1).to_broadcast([P, c1 - c0, P, 4]),
+                        op=ALU.mult,
+                    )
+                else:
+                    nc.vector.tensor_tensor(
+                        out=dst.rearrange("p (n i t) -> p n i t", n=c1 - c0, t=4),
+                        in0=rl[:].rearrange("p t (i n) -> p n i t", n=NL)[:, c0 - 1 - NG : c1 - 1 - NG],
+                        in1=l_scal[:].unsqueeze(1).unsqueeze(1).to_broadcast([P, c1 - c0, P, 4]),
+                        op=ALU.mult,
+                    )
+            if step > 0:
+                c0, c1 = PIECES[step - 1]
                 nc.vector.quantize_mx(
-                    out=wc[:, lo // 4 : hi // 4].bitcast(E4X4), scales=ws[:, lo // 4 : hi // 4], in_=grp[:, lo:hi]
+                    out=wc[:, c0 * P : c1 * P].bitcast(E4X4),
+                    scales=ws[:, c0 * P : c1 * P],
+                    in_=grp[:, c0 * P * 4 : c1 * P * 4],
                 )
-            quant[ic] = (wc, ws)
 
         with tc.tile_pool(name="prep", bufs=1) as prep:
             g_sb = prep.tile([P, 8, 512], BF16, name="g_sb")
@@ -151,7 +161,8 @@ def tile_kanlinear_kernel(
             nc.vector.tensor_tensor(
                 out=t_bias[:], in0=a_nhalf[:], in1=b_sb[:].rearrange("p c n -> p (c n)"), op=ALU.mult
             )
-            prep_weights(0)
+            for step in range(N_STEPS):
+                prep_weights(0, step)
 
         work = ctx.enter_context(tc.tile_pool(name="work", bufs=2))
         planes = {}
@@ -236,8 +247,11 @@ def tile_kanlinear_kernel(
 
         def emit_mx(job):
             ic, rh, u = job
-            wc, ws = quant[ic]
+            wc = quant[ic][0]
+            ws = quant[ic][1]
             chs = units[u][0]
+            if len(chs) == 1:
+                chs = (chs[0], chs[0])
             bank = psum.tile([P, HALF], F32, tag="mx", name="bank")
             for j, ch in enumerate(chs):
                 nc.tensor.matmul_mx(
@@ -246,18 +260,19 @@ def tile_kanlinear_kernel(
                     lhsT_scale=ws[:, ch * P : (ch + 1) * P],
                     rhs=g_codes[:, rh * HALF : (rh + 1) * HALF].bitcast(E5X4),
                     rhs_scale=g_scales[:, rh * HALF : (rh + 1) * HALF],
-                    start=(j == 0),
-                    stop=(j == len(chs) - 1),
+                    start=(j == 0 or chs[0] == chs[1]),
+                    stop=(j == 1 or chs[0] == chs[1]),
                 )
             banks[job] = bank
 
         def emit_prod(job):
             ic, rh, u = job
             if rh == 0 and u == 0 and ic + 1 < 4:
-                prep_weights(ic + 1)
+                new_planes(ic + 1)
                 if ic + 2 < 4:
                     load_weights(ic + 2)
-                new_planes(ic + 1)
+            if rh == 0 and u % 3 == 0 and u // 3 < N_STEPS and ic + 1 < 4:
+                prep_weights(ic + 1, u // 3)
             fam = units[u][1]
             idx = units[u][2]
             scal = units[u][3]

@@ -22,8 +22,6 @@ HALF = 512
 BUNCH = 2
 LOOK = 2
 N_AFFINE_ON_SCALAR = 8
-PIECES = ((0, 1), (1, 5), (5, 9), (9, 13), (13, 17), (17, 19))
-N_STEPS = len(PIECES) + 1
 FLOPS = 2 * ROWS * 512 * (FEAT * NCH)
 
 
@@ -76,42 +74,36 @@ def tile_kanlinear_kernel(
             )
             raw[ic] = (rb, ss, rs, rl)
 
-        def prep_weights(ic, step):
+        def prep_weights(ic):
             rb, ss, rs, rl = raw[ic]
-            if step == 0:
-                grp_new = wts.tile([P, NCH * P * 4], BF16, tag="grp", name="grp_new", bufs=1, align_bytes=64)
-                wc_new = wts.tile([P, NCH * P], U32, tag="wc", name="wc_new", align_bytes=64)
-                ws_new = wts.tile([P, NCH * P], U8, tag="ws", name="ws_new", align_bytes=64)
-                quant[ic] = (wc_new, ws_new, grp_new)
-            wc, ws, grp = quant[ic]
-            if step < len(PIECES):
-                c0, c1 = PIECES[step]
-                dst = grp[:, c0 * P * 4 : c1 * P * 4]
-                if c0 == 0:
-                    nc.vector.tensor_copy(
-                        out=dst.rearrange("p (i t) -> p i t", t=4), in_=rb[:].rearrange("p t i -> p i t")
-                    )
-                elif c0 < 1 + NG:
-                    nc.vector.tensor_tensor(
-                        out=dst.rearrange("p (g i t) -> p g i t", g=c1 - c0, t=4),
-                        in0=rs[:].rearrange("p t (i g) -> p g i t", g=NG)[:, c0 - 1 : c1 - 1],
-                        in1=ss[:].rearrange("p t i -> p i t").unsqueeze(1).to_broadcast([P, c1 - c0, P, 4]),
-                        op=ALU.mult,
-                    )
-                else:
-                    nc.vector.tensor_tensor(
-                        out=dst.rearrange("p (n i t) -> p n i t", n=c1 - c0, t=4),
-                        in0=rl[:].rearrange("p t (i n) -> p n i t", n=NL)[:, c0 - 1 - NG : c1 - 1 - NG],
-                        in1=l_scal[:].unsqueeze(1).unsqueeze(1).to_broadcast([P, c1 - c0, P, 4]),
-                        op=ALU.mult,
-                    )
-            if step > 0:
-                c0, c1 = PIECES[step - 1]
-                nc.vector.quantize_mx(
-                    out=wc[:, c0 * P : c1 * P].bitcast(E4X4),
-                    scales=ws[:, c0 * P : c1 * P],
-                    in_=grp[:, c0 * P * 4 : c1 * P * 4],
+            grp = wts.tile([P, NCH * P * 4], BF16, tag="grp", name="grp", bufs=1, align_bytes=64)
+            wc = wts.tile([P, NCH * P], U32, tag="wc", name="wc", align_bytes=64)
+            ws = wts.tile([P, NCH * P], U8, tag="ws", name="ws", align_bytes=64)
+            e0 = P * 4
+            e1 = e0 + NG * P * 4
+            e2 = e1 + NL * P * 4
+            nc.scalar.copy(
+                out=grp[:, 0:e0].rearrange("p (i t) -> p i t", t=4), in_=rb[:].rearrange("p t i -> p i t")
+            )
+            nc.vector.tensor_tensor(
+                out=grp[:, e0:e1].rearrange("p (g i t) -> p g i t", g=NG, t=4),
+                in0=rs[:].rearrange("p t (i g) -> p g i t", g=NG),
+                in1=ss[:].rearrange("p t i -> p i t").unsqueeze(1).to_broadcast([P, NG, P, 4]),
+                op=ALU.mult,
+            )
+            for t in range(4):
+                nc.vector.tensor_scalar(
+                    out=rl[:, t, :], in0=rl[:, t, :], scalar1=l_scal[:, t : t + 1], scalar2=None, op0=ALU.mult
                 )
+            nc.scalar.copy(
+                out=grp[:, e1:e2].rearrange("p (n i t) -> p n i t", n=NL, t=4),
+                in_=rl[:].rearrange("p t (i n) -> p n i t", n=NL),
+            )
+            for lo, hi in ((0, e0), (e0, e1), (e1, e1 + 4096), (e1 + 4096, e2)):
+                nc.vector.quantize_mx(
+                    out=wc[:, lo // 4 : hi // 4].bitcast(E4X4), scales=ws[:, lo // 4 : hi // 4], in_=grp[:, lo:hi]
+                )
+            quant[ic] = (wc, ws)
 
         with tc.tile_pool(name="prep", bufs=1) as prep:
             g_sb = prep.tile([P, 8, 512], BF16, name="g_sb")
@@ -161,8 +153,7 @@ def tile_kanlinear_kernel(
             nc.vector.tensor_tensor(
                 out=t_bias[:], in0=a_nhalf[:], in1=b_sb[:].rearrange("p c n -> p (c n)"), op=ALU.mult
             )
-            for step in range(N_STEPS):
-                prep_weights(0, step)
+            prep_weights(0)
 
         work = ctx.enter_context(tc.tile_pool(name="work", bufs=2))
         planes = {}
@@ -247,11 +238,8 @@ def tile_kanlinear_kernel(
 
         def emit_mx(job):
             ic, rh, u = job
-            wc = quant[ic][0]
-            ws = quant[ic][1]
+            wc, ws = quant[ic]
             chs = units[u][0]
-            if len(chs) == 1:
-                chs = (chs[0], chs[0])
             bank = psum.tile([P, HALF], F32, tag="mx", name="bank")
             for j, ch in enumerate(chs):
                 nc.tensor.matmul_mx(
@@ -260,19 +248,18 @@ def tile_kanlinear_kernel(
                     lhsT_scale=ws[:, ch * P : (ch + 1) * P],
                     rhs=g_codes[:, rh * HALF : (rh + 1) * HALF].bitcast(E5X4),
                     rhs_scale=g_scales[:, rh * HALF : (rh + 1) * HALF],
-                    start=(j == 0 or chs[0] == chs[1]),
-                    stop=(j == 1 or chs[0] == chs[1]),
+                    start=(j == 0),
+                    stop=(j == len(chs) - 1),
                 )
             banks[job] = bank
 
         def emit_prod(job):
             ic, rh, u = job
             if rh == 0 and u == 0 and ic + 1 < 4:
-                new_planes(ic + 1)
+                prep_weights(ic + 1)
                 if ic + 2 < 4:
                     load_weights(ic + 2)
-            if rh == 0 and u % 3 == 0 and u // 3 < N_STEPS and ic + 1 < 4:
-                prep_weights(ic + 1, u // 3)
+                new_planes(ic + 1)
             fam = units[u][1]
             idx = units[u][2]
             scal = units[u][3]

@@ -21,7 +21,8 @@ NCH = 1 + NG + NL
 HALF = 512
 BUNCH = 2
 LOOK = 2
-N_AFFINE_ON_SCALAR = 8
+N_DIAG = 7
+N_AFFINE_ON_SCALAR = 10
 FLOPS = 2 * ROWS * 512 * (FEAT * NCH)
 
 
@@ -91,13 +92,11 @@ def tile_kanlinear_kernel(
                 in1=ss[:].rearrange("p t i -> p i t").unsqueeze(1).to_broadcast([P, NG, P, 4]),
                 op=ALU.mult,
             )
-            for t in range(4):
-                nc.vector.tensor_scalar(
-                    out=rl[:, t, :], in0=rl[:, t, :], scalar1=l_scal[:, t : t + 1], scalar2=None, op0=ALU.mult
-                )
-            nc.scalar.copy(
+            nc.vector.tensor_tensor(
                 out=grp[:, e1:e2].rearrange("p (n i t) -> p n i t", n=NL, t=4),
-                in_=rl[:].rearrange("p t (i n) -> p n i t", n=NL),
+                in0=rl[:].rearrange("p t (i n) -> p n i t", n=NL),
+                in1=l_scal[:].unsqueeze(1).unsqueeze(1).to_broadcast([P, NL, P, 4]),
+                op=ALU.mult,
             )
             for lo, hi in ((0, e0), (e0, e1), (e1, e1 + 4096), (e1 + 4096, e2)):
                 nc.vector.quantize_mx(
@@ -105,57 +104,60 @@ def tile_kanlinear_kernel(
                 )
             quant[ic] = (wc, ws)
 
-        with tc.tile_pool(name="prep", bufs=1) as prep:
-            g_sb = prep.tile([P, 8, 512], BF16, name="g_sb")
-            nc.sync.dma_start(out=g_sb[:], in_=grad_out.rearrange("(t p) o -> p t o", p=P))
-            x_sb = prep.tile([P, 8, FEAT], BF16, name="x_sb")
-            nc.sync.dma_start(out=x_sb[:], in_=x.rearrange("(t p) i -> p t i", p=P))
-            ls_rows = prep.tile([P, P], BF16, name="ls_rows")
-            nc.vector.memset(ls_rows[:], 0.0)
-            nc.sync.dma_start(out=ls_rows[0:4, :], in_=logistic_scaler.rearrange("(t p) -> t p", p=P))
-            nc.sync.dma_start(out=a_sb[:], in_=a.rearrange("(c p) n -> p c n", p=P))
-            nc.sync.dma_start(out=b_sb[:], in_=b.rearrange("(c p) n -> p c n", p=P))
-            load_weights(0)
-            load_weights(1)
+        work = ctx.enter_context(tc.tile_pool(name="work", bufs=2))
 
-            ls_ps = psum.tile([P, P], BF16, tag="mx", name="ls_ps")
-            nc.tensor.transpose(ls_ps[:], ls_rows[:], ident_b[:])
-            nc.vector.tensor_copy(out=l_scal[:], in_=ls_ps[:, 0:4])
+        x_sb = wts.tile([P, 8, FEAT], BF16, tag="rl", name="x_sb")
+        nc.sync.dma_start(out=x_sb[:], in_=x.rearrange("(t p) i -> p t i", p=P))
+        nc.sync.dma_start(out=a_sb[:], in_=a.rearrange("(c p) n -> p c n", p=P))
+        nc.sync.dma_start(out=b_sb[:], in_=b.rearrange("(c p) n -> p c n", p=P))
+        ls_rows = const.tile([P, P], BF16, name="ls_rows")
+        nc.vector.memset(ls_rows[:], 0.0)
+        nc.sync.dma_start(out=ls_rows[0:4, :], in_=logistic_scaler.rearrange("(t p) -> t p", p=P))
+        load_weights(0)
+        g_sb = wts.tile([P, 8, 512], BF16, tag="rs", name="g_sb")
+        nc.sync.dma_start(out=g_sb[:], in_=grad_out.rearrange("(t p) o -> p t o", p=P))
+        load_weights(1)
 
-            gg = prep.tile([P, ROWS, 4], BF16, name="gg", align_bytes=64)
+        for ic in range(4):
+            px = psum.tile([P, 8, P], BF16, tag="mx", name="px")
             for rt in range(8):
-                pt = psum.tile([P, 4, P], BF16, tag="mx", name="pt")
-                for t in range(4):
-                    nc.tensor.transpose(pt[:, t, :], g_sb[:, rt, t * P : (t + 1) * P], ident_b[:])
-                if rt % 2 == 0:
-                    nc.vector.tensor_copy(out=gg[:, rt * P : (rt + 1) * P, :], in_=pt[:].rearrange("p t r -> p r t"))
-                else:
-                    nc.scalar.copy(out=gg[:, rt * P : (rt + 1) * P, :], in_=pt[:].rearrange("p t r -> p r t"))
+                nc.tensor.transpose(px[:, rt, :], x_sb[:, rt, ic * P : (ic + 1) * P], ident_b[:])
+            nc.scalar.copy(out=x_t[:, ic, :], in_=px[:].rearrange("p t r -> p (t r)"))
+
+        nc.vector.tensor_scalar(
+            out=a_half[:], in0=a_sb[:].rearrange("p c n -> p (c n)"), scalar1=0.5, scalar2=None, op0=ALU.mult
+        )
+        nc.vector.tensor_scalar(
+            out=a_nhalf[:], in0=a_sb[:].rearrange("p c n -> p (c n)"), scalar1=-0.5, scalar2=None, op0=ALU.mult
+        )
+        nc.vector.tensor_tensor(
+            out=t_bias[:], in0=a_nhalf[:], in1=b_sb[:].rearrange("p c n -> p (c n)"), op=ALU.mult
+        )
+
+        ls_ps = psum.tile([P, P], BF16, tag="mx", name="ls_ps")
+        nc.tensor.transpose(ls_ps[:], ls_rows[:], ident_b[:])
+        nc.vector.tensor_copy(out=l_scal[:], in_=ls_ps[:, 0:4])
+
+        def prep_grad():
             for rh in range(2):
+                gg = work.tile([P, HALF, 4], BF16, tag=("sp", "lg")[rh], name="gg", bufs=11, align_bytes=64)
+                for rq in range(4):
+                    rt = rh * 4 + rq
+                    pt = psum.tile([P, 4, P], BF16, tag="mx", name="pt")
+                    for t in range(4):
+                        nc.tensor.transpose(pt[:, t, :], g_sb[:, rt, t * P : (t + 1) * P], ident_b[:])
+                    if rq % 2 == 0:
+                        nc.vector.tensor_copy(
+                            out=gg[:, rq * P : (rq + 1) * P, :], in_=pt[:].rearrange("p t r -> p r t")
+                        )
+                    else:
+                        nc.scalar.copy(out=gg[:, rq * P : (rq + 1) * P, :], in_=pt[:].rearrange("p t r -> p r t"))
                 nc.vector.quantize_mx(
                     out=g_codes[:, rh * HALF : (rh + 1) * HALF].bitcast(E5X4),
                     scales=g_scales[:, rh * HALF : (rh + 1) * HALF],
-                    in_=gg[:, rh * HALF : (rh + 1) * HALF, :].rearrange("p r t -> p (r t)"),
+                    in_=gg[:].rearrange("p r t -> p (r t)"),
                 )
 
-            for ic in range(4):
-                px = psum.tile([P, 8, P], BF16, tag="mx", name="px")
-                for rt in range(8):
-                    nc.tensor.transpose(px[:, rt, :], x_sb[:, rt, ic * P : (ic + 1) * P], ident_b[:])
-                nc.scalar.copy(out=x_t[:, ic, :], in_=px[:].rearrange("p t r -> p (t r)"))
-
-            nc.vector.tensor_scalar(
-                out=a_half[:], in0=a_sb[:].rearrange("p c n -> p (c n)"), scalar1=0.5, scalar2=None, op0=ALU.mult
-            )
-            nc.vector.tensor_scalar(
-                out=a_nhalf[:], in0=a_sb[:].rearrange("p c n -> p (c n)"), scalar1=-0.5, scalar2=None, op0=ALU.mult
-            )
-            nc.vector.tensor_tensor(
-                out=t_bias[:], in0=a_nhalf[:], in1=b_sb[:].rearrange("p c n -> p (c n)"), op=ALU.mult
-            )
-            prep_weights(0)
-
-        work = ctx.enter_context(tc.tile_pool(name="work", bufs=2))
         planes = {}
 
         def merge(dst, src):
@@ -166,9 +168,9 @@ def tile_kanlinear_kernel(
         def gen_spline(ic, m):
             xi = x_t[:, ic, :]
             mid = 0.4 * m - 1.8
-            c = work.tile([P, ROWS], F32, tag="sp", name="c", bufs=11)
+            c = work.tile([P, ROWS], F32, tag="sp", name="c", bufs=11, align_bytes=64)
             nc.vector.tensor_scalar(out=c[:], in0=xi, scalar1=mid - 0.4, scalar2=mid + 0.4, op0=ALU.max, op1=ALU.min)
-            ab = work.tile([P, ROWS], F32, tag="ab", name="ab", bufs=3)
+            ab = work.tile([P, ROWS], F32, tag="ab", name="ab", bufs=2)
             nc.scalar.activation(out=ab[:], in_=c[:], func=ACT.Abs, bias=4.5 - m, scale=2.5)
             nc.scalar.activation(out=ab[:], in_=ab[:], func=ACT.Identity, bias=-5.0, scale=2.5)
             nc.vector.scalar_tensor_tensor(
@@ -186,12 +188,18 @@ def tile_kanlinear_kernel(
 
         def gen_logistic(ic, n):
             k = ic * NL + n
-            t = work.tile([P, ROWS], F32, tag="lg", name="t", bufs=11)
+            t = work.tile([P, ROWS], F32, tag="lg", name="t", bufs=11, align_bytes=64)
             nc.scalar.activation(
                 out=t[:], in_=x_t[:, ic, :], func=ACT.Tanh, bias=t_bias[:, k : k + 1], scale=a_half[:, k : k + 1]
             )
             nc.scalar.activation(out=t[:], in_=t[:], func=ACT.Square)
-            if n < N_AFFINE_ON_SCALAR:
+            if n < N_DIAG:
+                dg = planes[ic]["dg"]
+                nc.gpsimd.tensor_scalar(
+                    out=dg[:, n, :], in0=ident_f[:], scalar1=a_nhalf[:, k : k + 1], scalar2=0.0,
+                    op0=ALU.mult, op1=ALU.add,
+                )
+            elif n < N_AFFINE_ON_SCALAR:
                 nc.scalar.activation(
                     out=t[:], in_=t[:], func=ACT.Identity, bias=a_half[:, k : k + 1], scale=a_nhalf[:, k : k + 1]
                 )
@@ -208,7 +216,7 @@ def tile_kanlinear_kernel(
             nc.scalar.activation(out=th[:], in_=xi, func=ACT.Tanh, scale=0.5)
             ds = work.tile([P, ROWS], F32, tag="ds", name="ds", bufs=2)
             nc.scalar.activation(out=ds[:], in_=th[:], func=ACT.Square)
-            nc.vector.tensor_scalar(out=ds[:], in0=ds[:], scalar1=-0.25, scalar2=0.25, op0=ALU.mult, op1=ALU.add)
+            nc.scalar.activation(out=ds[:], in_=ds[:], func=ACT.Identity, bias=0.25, scale=-0.25)
             nc.vector.tensor_tensor(out=ds[:], in0=ds[:], in1=xi, op=ALU.mult)
             nc.vector.scalar_tensor_tensor(
                 out=ds[:], in0=th[:], scalar=0.5, in1=ds[:], op0=ALU.mult, op1=ALU.add
@@ -216,17 +224,21 @@ def tile_kanlinear_kernel(
             planes[ic]["ds"] = ds
 
         def new_planes(ic):
-            planes[ic] = {"sp": [None] * 10, "lg": [None] * NL, "ds": None}
+            dg_new = work.tile([P, N_DIAG, P], F32, tag="dg", name="dg_new", bufs=2)
+            planes[ic] = {"sp": [None] * 10, "lg": [None] * NL, "ds": None, "dg": dg_new}
 
-        units = [((1, ), "sp", 0, -1.25, 0), ((2, ), "sp", 1, -1.25, 1), ((3, 1), "sp", 2, -1.25, 2)]
+        spline_units = [((1, ), "sp", 0, -1.25, 0), ((2, ), "sp", 1, -1.25, 1), ((3, 1), "sp", 2, -1.25, 2)]
         for m in range(3, 7):
-            units.append(((1 + m, m - 1), "sp", m, -1.25, None))
-            units.append(((m, ), "sp", m, 2.5, m))
-        units.append(((8, 6), "sp", 7, -1.25, 7))
-        units.append(((7, ), "sp", 8, -1.25, 8))
-        units.append(((8, ), "sp", 9, -1.25, 9))
-        for n in range(NL):
-            units.append(((1 + NG + n, ), "lg", n, None, n))
+            spline_units.append(((1 + m, m - 1), "sp", m, -1.25, None))
+            spline_units.append(((m, ), "sp", m, 2.5, m))
+        spline_units.append(((8, 6), "sp", 7, -1.25, 7))
+        spline_units.append(((7, ), "sp", 8, -1.25, 8))
+        spline_units.append(((8, ), "sp", 9, -1.25, 9))
+        units = []
+        for k in range(len(spline_units)):
+            units.append(spline_units[k])
+            if k < NL:
+                units.append(((1 + NG + k, ), "lg", k, None, k))
         units.append(((0, ), "ds", 0, 0.5, 0))
         n_units = len(units)
 
@@ -270,6 +282,11 @@ def tile_kanlinear_kernel(
                 nc.vector.scalar_tensor_tensor(
                     out=y[:], in0=planes[ic]["sp"][idx][:, cols], scalar=scal, in1=bank[:], op0=ALU.mult, op1=ALU.mult
                 )
+            elif fam == "lg" and idx < N_DIAG:
+                nc.vector.scalar_tensor_tensor(
+                    out=y[:], in0=planes[ic]["lg"][idx][:, cols], scalar=1.0, in1=bank[:],
+                    op0=ALU.subtract, op1=ALU.mult,
+                )
             elif fam == "lg":
                 nc.vector.tensor_tensor(out=y[:], in0=bank[:], in1=planes[ic]["lg"][idx][:, cols], op=ALU.mult)
             else:
@@ -293,15 +310,25 @@ def tile_kanlinear_kernel(
                 acc_new = psacc.tile([P, HALF], F32, tag="acc%d" % rh, name="acc_new")
                 accs[(ic, rh)] = acc_new
             acc = accs[(ic, rh)]
+            scaled = units[u][1] == "lg" and units[u][2] < N_DIAG
             for rt in range(4):
-                nc.tensor.matmul(
-                    out=acc[:, rt * P : (rt + 1) * P],
-                    lhsT=y[:, rt * P : (rt + 1) * P],
-                    rhs=ident_f[:],
-                    is_transpose=True,
-                    start=(u == 0 and rt == 0),
-                    stop=(u == n_units - 1 and rt == 3),
-                )
+                if scaled:
+                    nc.tensor.matmul(
+                        out=acc[:, rt * P : (rt + 1) * P],
+                        lhsT=y[:, rt * P : (rt + 1) * P],
+                        rhs=planes[ic]["dg"][:, units[u][2], :],
+                        start=False,
+                        stop=False,
+                    )
+                else:
+                    nc.tensor.matmul(
+                        out=acc[:, rt * P : (rt + 1) * P],
+                        lhsT=y[:, rt * P : (rt + 1) * P],
+                        rhs=ident_f[:],
+                        is_transpose=True,
+                        start=(u == 0 and rt == 0),
+                        stop=(u == n_units - 1 and rt == 3),
+                    )
             if u == n_units - 1:
                 ob = work.tile([P, 4, P], F32, tag="ob", name="ob", bufs=2)
                 nc.scalar.copy(out=ob[:].rearrange("p t i -> p (t i)"), in_=acc[:])
@@ -312,9 +339,10 @@ def tile_kanlinear_kernel(
 
         new_planes(0)
         for m in range(10):
+            gen_logistic(0, m)
             gen_spline(0, m)
-        for n in range(NL):
-            gen_logistic(0, n)
+        prep_weights(0)
+        prep_grad()
         gen_base(0)
 
         for k in range(LOOK):

from contextlib import ExitStack

import concourse.mybir as mybir
from concourse.masks import make_identity

F32 = mybir.dt.float32
BF16 = mybir.dt.bfloat16
U32 = mybir.dt.uint32
U8 = mybir.dt.uint8
E4X4 = mybir.dt.float8_e4m3fn_x4
E5X4 = mybir.dt.float8_e5m2_x4
ALU = mybir.AluOpType
ACT = mybir.ActivationFunctionType

P = 128
ROWS = 1024
FEAT = 512
NG = 8
NL = 10
NCH = 1 + NG + NL
HALF = 512
BUNCH = 2
LOOK = 2
N_DIAG = 7
N_AFFINE_ON_SCALAR = 10
FLOPS = 2 * ROWS * 512 * (FEAT * NCH)


def tile_kanlinear_kernel(
    tc, x, base_weight, spline_weight, spline_scaler, a, b, logistic_weight, logistic_scaler, grad_out, out
):
    nc = tc.nc
    with ExitStack() as ctx:
        const = ctx.enter_context(tc.tile_pool(name="const", bufs=1))
        wts = ctx.enter_context(tc.tile_pool(name="wts", bufs=2))
        psum = ctx.enter_context(tc.psum_pool(name="psum", bufs=6))
        psacc = ctx.enter_context(tc.psum_pool(name="psacc", bufs=1))

        ident_b = const.tile([P, P], BF16, name="ident_b")
        make_identity(nc, ident_b[:])
        ident_f = const.tile([P, P], F32, name="ident_f")
        make_identity(nc, ident_f[:])

        x_t = const.tile([P, 4, ROWS], F32, name="x_t")
        g_codes = const.tile([P, ROWS], U32, name="g_codes", align_bytes=64)
        g_scales = const.tile([P, ROWS], U8, name="g_scales", align_bytes=64)
        a_sb = const.tile([P, 4, NL], BF16, name="a_sb")
        b_sb = const.tile([P, 4, NL], BF16, name="b_sb")
        a_half = const.tile([P, 4 * NL], F32, name="a_half")
        a_nhalf = const.tile([P, 4 * NL], F32, name="a_nhalf")
        t_bias = const.tile([P, 4 * NL], F32, name="t_bias")
        l_scal = const.tile([P, 4], BF16, name="l_scal")

        raw = {}
        quant = {}

        def load_weights(ic):
            rb = wts.tile([P, 4, P], BF16, tag="rb", name="rb")
            nc.sync.dma_start(
                out=rb[:], in_=base_weight.rearrange("(t p) i -> p t i", p=P)[:, :, ic * P : (ic + 1) * P]
            )
            ss = wts.tile([P, 4, P], BF16, tag="ss", name="ss")
            nc.sync.dma_start(
                out=ss[:], in_=spline_scaler.rearrange("(t p) i -> p t i", p=P)[:, :, ic * P : (ic + 1) * P]
            )
            rs = wts.tile([P, 4, P * NG], BF16, tag="rs", name="rs")
            nc.sync.dma_start(
                out=rs[:],
                in_=spline_weight.rearrange("(t p) i g -> p t (i g)", p=P)[:, :, ic * P * NG : (ic + 1) * P * NG],
            )
            rl = wts.tile([P, 4, P * NL], BF16, tag="rl", name="rl")
            nc.sync.dma_start(
                out=rl[:],
                in_=logistic_weight.rearrange("(t p) c -> p t c", p=P)[:, :, ic * P * NL : (ic + 1) * P * NL],
            )
            raw[ic] = (rb, ss, rs, rl)

        def prep_weights(ic):
            rb, ss, rs, rl = raw[ic]
            grp = wts.tile([P, NCH * P * 4], BF16, tag="grp", name="grp", bufs=1, align_bytes=64)
            wc = wts.tile([P, NCH * P], U32, tag="wc", name="wc", align_bytes=64)
            ws = wts.tile([P, NCH * P], U8, tag="ws", name="ws", align_bytes=64)
            e0 = P * 4
            e1 = e0 + NG * P * 4
            e2 = e1 + NL * P * 4
            nc.scalar.copy(
                out=grp[:, 0:e0].rearrange("p (i t) -> p i t", t=4), in_=rb[:].rearrange("p t i -> p i t")
            )
            nc.vector.tensor_tensor(
                out=grp[:, e0:e1].rearrange("p (g i t) -> p g i t", g=NG, t=4),
                in0=rs[:].rearrange("p t (i g) -> p g i t", g=NG),
                in1=ss[:].rearrange("p t i -> p i t").unsqueeze(1).to_broadcast([P, NG, P, 4]),
                op=ALU.mult,
            )
            nc.vector.tensor_tensor(
                out=grp[:, e1:e2].rearrange("p (n i t) -> p n i t", n=NL, t=4),
                in0=rl[:].rearrange("p t (i n) -> p n i t", n=NL),
                in1=l_scal[:].unsqueeze(1).unsqueeze(1).to_broadcast([P, NL, P, 4]),
                op=ALU.mult,
            )
            for lo, hi in ((0, e0), (e0, e1), (e1, e1 + 4096), (e1 + 4096, e2)):
                nc.vector.quantize_mx(
                    out=wc[:, lo // 4 : hi // 4].bitcast(E4X4), scales=ws[:, lo // 4 : hi // 4], in_=grp[:, lo:hi]
                )
            quant[ic] = (wc, ws)

        work = ctx.enter_context(tc.tile_pool(name="work", bufs=2))

        x_sb = wts.tile([P, 8, FEAT], BF16, tag="rl", name="x_sb")
        nc.sync.dma_start(out=x_sb[:], in_=x.rearrange("(t p) i -> p t i", p=P))
        nc.sync.dma_start(out=a_sb[:], in_=a.rearrange("(c p) n -> p c n", p=P))
        nc.sync.dma_start(out=b_sb[:], in_=b.rearrange("(c p) n -> p c n", p=P))
        ls_rows = const.tile([P, P], BF16, name="ls_rows")
        nc.vector.memset(ls_rows[:], 0.0)
        nc.sync.dma_start(out=ls_rows[0:4, :], in_=logistic_scaler.rearrange("(t p) -> t p", p=P))
        load_weights(0)
        g_sb = wts.tile([P, 8, 512], BF16, tag="rs", name="g_sb")
        nc.sync.dma_start(out=g_sb[:], in_=grad_out.rearrange("(t p) o -> p t o", p=P))
        load_weights(1)

        for ic in range(4):
            px = psum.tile([P, 8, P], BF16, tag="mx", name="px")
            for rt in range(8):
                nc.tensor.transpose(px[:, rt, :], x_sb[:, rt, ic * P : (ic + 1) * P], ident_b[:])
            nc.scalar.copy(out=x_t[:, ic, :], in_=px[:].rearrange("p t r -> p (t r)"))

        nc.vector.tensor_scalar(
            out=a_half[:], in0=a_sb[:].rearrange("p c n -> p (c n)"), scalar1=0.5, scalar2=None, op0=ALU.mult
        )
        nc.vector.tensor_scalar(
            out=a_nhalf[:], in0=a_sb[:].rearrange("p c n -> p (c n)"), scalar1=-0.5, scalar2=None, op0=ALU.mult
        )
        nc.vector.tensor_tensor(
            out=t_bias[:], in0=a_nhalf[:], in1=b_sb[:].rearrange("p c n -> p (c n)"), op=ALU.mult
        )

        ls_ps = psum.tile([P, P], BF16, tag="mx", name="ls_ps")
        nc.tensor.transpose(ls_ps[:], ls_rows[:], ident_b[:])
        nc.vector.tensor_copy(out=l_scal[:], in_=ls_ps[:, 0:4])

        def prep_grad():
            for rh in range(2):
                gg = work.tile([P, HALF, 4], BF16, tag=("sp", "lg")[rh], name="gg", bufs=11, align_bytes=64)
                for rq in range(4):
                    rt = rh * 4 + rq
                    pt = psum.tile([P, 4, P], BF16, tag="mx", name="pt")
                    for t in range(4):
                        nc.tensor.transpose(pt[:, t, :], g_sb[:, rt, t * P : (t + 1) * P], ident_b[:])
                    if rq % 2 == 0:
                        nc.vector.tensor_copy(
                            out=gg[:, rq * P : (rq + 1) * P, :], in_=pt[:].rearrange("p t r -> p r t")
                        )
                    else:
                        nc.scalar.copy(out=gg[:, rq * P : (rq + 1) * P, :], in_=pt[:].rearrange("p t r -> p r t"))
                nc.vector.quantize_mx(
                    out=g_codes[:, rh * HALF : (rh + 1) * HALF].bitcast(E5X4),
                    scales=g_scales[:, rh * HALF : (rh + 1) * HALF],
                    in_=gg[:].rearrange("p r t -> p (r t)"),
                )

        planes = {}

        def merge(dst, src):
            nc.vector.scalar_tensor_tensor(
                out=dst[:], in0=src[:], scalar=-2.0, in1=dst[:], op0=ALU.mult, op1=ALU.add
            )

        def gen_spline(ic, m):
            xi = x_t[:, ic, :]
            mid = 0.4 * m - 1.8
            c = work.tile([P, ROWS], F32, tag="sp", name="c", bufs=11, align_bytes=64)
            nc.vector.tensor_scalar(out=c[:], in0=xi, scalar1=mid - 0.4, scalar2=mid + 0.4, op0=ALU.max, op1=ALU.min)
            ab = work.tile([P, ROWS], F32, tag="ab", name="ab", bufs=2)
            nc.scalar.activation(out=ab[:], in_=c[:], func=ACT.Abs, bias=4.5 - m, scale=2.5)
            nc.scalar.activation(out=ab[:], in_=ab[:], func=ACT.Identity, bias=-5.0, scale=2.5)
            nc.vector.scalar_tensor_tensor(
                out=c[:], in0=c[:], scalar=mid, in1=ab[:], op0=ALU.subtract, op1=ALU.mult
            )
            sp = planes[ic]["sp"]
            sp[m] = c
            if m == 1:
                merge(sp[0], sp[1])
            if m == 2:
                merge(sp[1], sp[2])
            if m == 9:
                merge(sp[9], sp[8])
                merge(sp[8], sp[7])

        def gen_logistic(ic, n):
            k = ic * NL + n
            t = work.tile([P, ROWS], F32, tag="lg", name="t", bufs=11, align_bytes=64)
            nc.scalar.activation(
                out=t[:], in_=x_t[:, ic, :], func=ACT.Tanh, bias=t_bias[:, k : k + 1], scale=a_half[:, k : k + 1]
            )
            nc.scalar.activation(out=t[:], in_=t[:], func=ACT.Square)
            if n < N_DIAG:
                dg = planes[ic]["dg"]
                nc.gpsimd.tensor_scalar(
                    out=dg[:, n, :], in0=ident_f[:], scalar1=a_nhalf[:, k : k + 1], scalar2=0.0,
                    op0=ALU.mult, op1=ALU.add,
                )
            elif n < N_AFFINE_ON_SCALAR:
                nc.scalar.activation(
                    out=t[:], in_=t[:], func=ACT.Identity, bias=a_half[:, k : k + 1], scale=a_nhalf[:, k : k + 1]
                )
            else:
                nc.vector.tensor_scalar(
                    out=t[:], in0=t[:], scalar1=a_nhalf[:, k : k + 1], scalar2=a_half[:, k : k + 1],
                    op0=ALU.mult, op1=ALU.add,
                )
            planes[ic]["lg"][n] = t

        def gen_base(ic):
            xi = x_t[:, ic, :]
            th = work.tile([P, ROWS], F32, tag="th", name="th", bufs=1)
            nc.scalar.activation(out=th[:], in_=xi, func=ACT.Tanh, scale=0.5)
            ds = work.tile([P, ROWS], F32, tag="ds", name="ds", bufs=2)
            nc.scalar.activation(out=ds[:], in_=th[:], func=ACT.Square)
            nc.scalar.activation(out=ds[:], in_=ds[:], func=ACT.Identity, bias=0.25, scale=-0.25)
            nc.vector.tensor_tensor(out=ds[:], in0=ds[:], in1=xi, op=ALU.mult)
            nc.vector.scalar_tensor_tensor(
                out=ds[:], in0=th[:], scalar=0.5, in1=ds[:], op0=ALU.mult, op1=ALU.add
            )
            planes[ic]["ds"] = ds

        def new_planes(ic):
            dg_new = work.tile([P, N_DIAG, P], F32, tag="dg", name="dg_new", bufs=2)
            planes[ic] = {"sp": [None] * 10, "lg": [None] * NL, "ds": None, "dg": dg_new}

        spline_units = [((1, ), "sp", 0, -1.25, 0), ((2, ), "sp", 1, -1.25, 1), ((3, 1), "sp", 2, -1.25, 2)]
        for m in range(3, 7):
            spline_units.append(((1 + m, m - 1), "sp", m, -1.25, None))
            spline_units.append(((m, ), "sp", m, 2.5, m))
        spline_units.append(((8, 6), "sp", 7, -1.25, 7))
        spline_units.append(((7, ), "sp", 8, -1.25, 8))
        spline_units.append(((8, ), "sp", 9, -1.25, 9))
        units = []
        for k in range(len(spline_units)):
            units.append(spline_units[k])
            if k < NL:
                units.append(((1 + NG + k, ), "lg", k, None, k))
        units.append(((0, ), "ds", 0, 0.5, 0))
        n_units = len(units)

        todo = [(ic, rh, u) for ic in range(4) for u in range(n_units) for rh in range(2)]
        bunches = [todo[k : k + BUNCH] for k in range(0, len(todo), BUNCH)]
        banks = {}
        prods = {}
        accs = {}

        def emit_mx(job):
            ic, rh, u = job
            wc, ws = quant[ic]
            chs = units[u][0]
            bank = psum.tile([P, HALF], F32, tag="mx", name="bank")
            for j, ch in enumerate(chs):
                nc.tensor.matmul_mx(
                    out=bank[:],
                    lhsT=wc[:, ch * P : (ch + 1) * P].bitcast(E4X4),
                    lhsT_scale=ws[:, ch * P : (ch + 1) * P],
                    rhs=g_codes[:, rh * HALF : (rh + 1) * HALF].bitcast(E5X4),
                    rhs_scale=g_scales[:, rh * HALF : (rh + 1) * HALF],
                    start=(j == 0),
                    stop=(j == len(chs) - 1),
                )
            banks[job] = bank

        def emit_prod(job):
            ic, rh, u = job
            if rh == 0 and u == 0 and ic + 1 < 4:
                prep_weights(ic + 1)
                if ic + 2 < 4:
                    load_weights(ic + 2)
                new_planes(ic + 1)
            fam = units[u][1]
            idx = units[u][2]
            scal = units[u][3]
            bank = banks[job]
            y = work.tile([P, HALF], F32, tag="y", name="y", bufs=6)
            cols = slice(rh * HALF, (rh + 1) * HALF)
            if fam == "sp":
                nc.vector.scalar_tensor_tensor(
                    out=y[:], in0=planes[ic]["sp"][idx][:, cols], scalar=scal, in1=bank[:], op0=ALU.mult, op1=ALU.mult
                )
            elif fam == "lg" and idx < N_DIAG:
                nc.vector.scalar_tensor_tensor(
                    out=y[:], in0=planes[ic]["lg"][idx][:, cols], scalar=1.0, in1=bank[:],
                    op0=ALU.subtract, op1=ALU.mult,
                )
            elif fam == "lg":
                nc.vector.tensor_tensor(out=y[:], in0=bank[:], in1=planes[ic]["lg"][idx][:, cols], op=ALU.mult)
            else:
                nc.vector.scalar_tensor_tensor(
                    out=y[:], in0=planes[ic]["ds"][:, cols], scalar=scal, in1=bank[:], op0=ALU.add, op1=ALU.mult
                )
            prods[job] = y
            freed = units[u][4]
            if rh == 1 and ic + 1 < 4 and freed is not None:
                if fam == "sp":
                    gen_spline(ic + 1, freed)
                elif fam == "lg":
                    gen_logistic(ic + 1, freed)
                else:
                    gen_base(ic + 1)

        def emit_acc(job):
            ic, rh, u = job
            y = prods[job]
            if u == 0:
                acc_new = psacc.tile([P, HALF], F32, tag="acc%d" % rh, name="acc_new")
                accs[(ic, rh)] = acc_new
            acc = accs[(ic, rh)]
            scaled = units[u][1] == "lg" and units[u][2] < N_DIAG
            for rt in range(4):
                if scaled:
                    nc.tensor.matmul(
                        out=acc[:, rt * P : (rt + 1) * P],
                        lhsT=y[:, rt * P : (rt + 1) * P],
                        rhs=planes[ic]["dg"][:, units[u][2], :],
                        start=False,
                        stop=False,
                    )
                else:
                    nc.tensor.matmul(
                        out=acc[:, rt * P : (rt + 1) * P],
                        lhsT=y[:, rt * P : (rt + 1) * P],
                        rhs=ident_f[:],
                        is_transpose=True,
                        start=(u == 0 and rt == 0),
                        stop=(u == n_units - 1 and rt == 3),
                    )
            if u == n_units - 1:
                ob = work.tile([P, 4, P], F32, tag="ob", name="ob", bufs=2)
                nc.scalar.copy(out=ob[:].rearrange("p t i -> p (t i)"), in_=acc[:])
                nc.sync.dma_start(
                    out=out.rearrange("(t p) i -> p t i", p=P)[:, rh * 4 : (rh + 1) * 4, ic * P : (ic + 1) * P],
                    in_=ob[:],
                )

        new_planes(0)
        for m in range(10):
            gen_logistic(0, m)
            gen_spline(0, m)
        prep_weights(0)
        prep_grad()
        gen_base(0)

        for k in range(LOOK):
            for job in bunches[k]:
                emit_mx(job)
        for k in range(len(bunches)):
            if k + LOOK < len(bunches):
                for job in bunches[k + LOOK]:
                    emit_mx(job)
            for job in bunches[k]:
                emit_prod(job)
            for job in bunches[k]:
                emit_acc(job)
